import numpy as np
import ml_dtypes


def mxq(x, axis, fmt="e4m3"):
    dtype, down = {"e4m3": (ml_dtypes.float8_e4m3fn, 7), "e5m2": (ml_dtypes.float8_e5m2, 14)}[fmt]
    v = np.moveaxis(np.asarray(x, np.float32).astype(ml_dtypes.bfloat16).astype(np.float64), axis, -1)
    blocks = v.reshape(v.shape[:-1] + (-1, 32))
    amax = np.abs(blocks).max(-1, keepdims=True)
    byte = np.maximum(np.where(amax > 0, np.frexp(amax)[1] - 1 + 127, 0) - down, 1)
    scale = np.exp2(byte - 127.0)
    codes = (blocks / scale).astype(np.float32).astype(dtype).astype(np.float64)
    return np.moveaxis((codes * scale).reshape(v.shape), -1, axis)


WIDE = False


def mx_kscale(k):
    if not WIDE:
        return np.ones(k)
    levels = np.array([10, -10, 5, -5, 0])
    a = np.random.permutation(np.resize(levels, k // 512 * 4)).reshape(k // 512, 4)
    idx = np.arange(k)
    return np.exp2(a[idx // 512, idx % 128 // 32])


BF16 = ml_dtypes.bfloat16


def bf(x):
    return np.asarray(x, np.float32).astype(BF16)


def f64(x):
    return np.asarray(x).astype(np.float64)


B, N, K, D, L = 1, 128, 16, 512, 128


def setup_inputs():
    s = mx_kscale(D)
    limit = np.sqrt(6.0 / (D + L))
    lone = np.random.random((B, N, 1)) < 0.125
    a = (0.3 + 0.7 * np.random.random((B, N, K + 1))) * np.where(lone, 0.4 / (K + 1), 1.0)
    return {"targets": bf(np.random.standard_normal((B, N, D)) * s),
            "neighbors": bf(np.random.standard_normal((B, N, K, D)) * s),
            "a": bf(a),
            "kernel": bf(np.random.uniform(-limit, limit, (D, L)) / s[:, None])}


def reference(targets, neighbors, a, kernel):
    neighborhood = np.concatenate([f64(targets)[..., None, :], f64(neighbors)], axis=-2)
    y = (mxq(neighborhood, 3, "e4m3") @ mxq(f64(kernel), 0, "e4m3")).sum(axis=-2)
    factor = f64(a).sum(axis=-1, keepdims=True)
    factor = np.where(factor > 0.5, factor, np.ones_like(factor))
    y = y / factor
    return np.maximum(y, 0.0)

@@ -1,0 +1,126 @@
+from contextlib import ExitStack
+
+import concourse.mybir as mybir
+from concourse.masks import make_identity
+
+F32 = mybir.dt.float32
+BF16 = mybir.dt.bfloat16
+U32 = mybir.dt.uint32
+U8 = mybir.dt.uint8
+FP8X4 = mybir.dt.float8_e4m3fn_x4
+ALU = mybir.AluOpType
+
+P = 128
+D = 512
+PACK = 4
+NEIGHBORS = 16
+MEMBERS = NEIGHBORS + 1
+WORDS = D // 2
+HALVES = WORDS // P
+BANK_MEMBERS = 2
+
+FLOPS = 2 * MEMBERS * P * D * P
+
+
+def tile_singlegcnlayer_s_kernel(tc, targets, neighbors, a, kernel, out):
+    nc = tc.nc
+    targets_rows = targets.rearrange("b n d -> (b n) d")
+    neighbor_rows = neighbors.rearrange("b n k d -> (b n) (k d)")
+    a_rows = a.rearrange("b n k -> (b n) k")
+    out_rows = out.rearrange("b n l -> (b n) l")
+
+    groups = [
+        neighbor_rows[:, first * D : (first + BANK_MEMBERS) * D]
+        for first in range(0, NEIGHBORS, BANK_MEMBERS)
+    ]
+    groups.append(targets_rows)
+
+    with ExitStack() as ctx:
+        consts = ctx.enter_context(tc.tile_pool(name="consts", bufs=1))
+        rows = ctx.enter_context(tc.tile_pool(name="rows", bufs=len(groups)))
+        staged = ctx.enter_context(tc.tile_pool(name="staged", bufs=len(groups)))
+        banks = ctx.enter_context(tc.psum_pool(name="banks", bufs=6))
+        sums = ctx.enter_context(tc.psum_pool(name="sums", bufs=1))
+
+        w_raw = consts.tile([P, PACK, P], BF16)
+        nc.scalar.dma_start(
+            out=w_raw[:].rearrange("p (u e) l -> p u (e l)", u=HALVES),
+            in_=kernel.rearrange("(u p e) l -> p u (e l)", u=HALVES, e=2),
+        )
+        a_sb = consts.tile([P, MEMBERS], BF16)
+        nc.scalar.dma_start(out=a_sb[:], in_=a_rows)
+
+        x_tiles = []
+        for group in groups:
+            x = rows.tile([P, group.shape[1]], BF16)
+            nc.sync.dma_start(out=x[:], in_=group)
+            x_tiles.append(x)
+
+        ident = consts.tile([P, P], F32)
+        make_identity(nc, ident[:])
+
+        w_grouped = consts.tile([P, P, PACK], BF16, align_bytes=64)
+        nc.vector.tensor_copy(out=w_grouped[:], in_=w_raw[:].rearrange("p t l -> p l t"))
+        w_codes = consts.tile([P, P], U32, align_bytes=64)
+        w_scales = consts.tile([P, P], U8, align_bytes=64)
+        nc.vector.quantize_mx(
+            out=w_codes[:].bitcast(FP8X4),
+            scales=w_scales[:],
+            in_=w_grouped[:].rearrange("p l t -> p (l t)"),
+        )
+
+        factor = consts.tile([P, 1], F32)
+        nc.vector.tensor_reduce(out=factor[:], in_=a_sb[:], axis=mybir.AxisListType.X, op=ALU.add)
+        small = consts.tile([P, 1], F32)
+        nc.vector.tensor_single_scalar(out=small[:], in_=factor[:], scalar=0.5, op=ALU.is_le)
+        guarded = consts.tile([P, 1], F32)
+        nc.vector.tensor_tensor(out=guarded[:], in0=factor[:], in1=small[:], op=ALU.max)
+        inverse = consts.tile([P, 1], F32)
+        nc.vector.reciprocal(out=inverse[:], in_=guarded[:])
+
+        y = sums.tile([P, P], F32)
+        passes_done = 0
+        for x in x_tiles:
+            members = x.shape[1] // D
+            x_words = x[:].bitcast(F32)
+
+            xt = banks.tile([P, members, HALVES, P], F32)
+            for m in range(members):
+                for u in range(HALVES):
+                    first_word = (m * HALVES + u) * P
+                    nc.tensor.transpose(
+                        xt[:, m, u, :], x_words[:, first_word : first_word + P], ident[:]
+                    )
+
+            grouped = staged.tile([P, members * P * PACK], BF16, align_bytes=64)
+            grouped_words = grouped[:].bitcast(F32).rearrange(
+                "p (m n u) -> p m n u", m=members, u=HALVES
+            )
+            xt_by_node = xt[:].rearrange("p m u n -> p m n u")
+            if members == BANK_MEMBERS:
+                nc.scalar.copy(out=grouped_words, in_=xt_by_node)
+            else:
+                nc.vector.tensor_copy(out=grouped_words, in_=xt_by_node)
+
+            codes = staged.tile([P, members * P], U32, align_bytes=64)
+            scales = staged.tile([P, members * P], U8, align_bytes=64)
+            nc.vector.quantize_mx(out=codes[:].bitcast(FP8X4), scales=scales[:], in_=grouped[:])
+
+            for m in range(members):
+                nodes = slice(m * P, (m + 1) * P)
+                nc.tensor.matmul_mx(
+                    out=y[:],
+                    lhsT=codes[:, nodes].bitcast(FP8X4),
+                    lhsT_scale=scales[:, nodes],
+                    rhs=w_codes[:].bitcast(FP8X4),
+                    rhs_scale=w_scales[:],
+                    start=(passes_done == 0),
+                    stop=(passes_done == MEMBERS - 1),
+                )
+                passes_done += 1
+
+        result = consts.tile([P, P], F32)
+        nc.vector.tensor_scalar(
+            out=result[:], in0=y[:], scalar1=inverse[:, 0:1], scalar2=0.0, op0=ALU.mult, op1=ALU.max
+        )
+        nc.sync.dma_start(out=out_rows, in_=result[:])

@@ -18,6 +18,7 @@ MEMBERS = NEIGHBORS + 1
 WORDS = D // 2
 HALVES = WORDS // P
 BANK_MEMBERS = 2
+BUNCH = 3
 
 FLOPS = 2 * MEMBERS * P * D * P
 
@@ -34,30 +35,75 @@ def tile_singlegcnlayer_s_kernel(tc, targets, neighbors, a, kernel, out):
         for first in range(0, NEIGHBORS, BANK_MEMBERS)
     ]
     groups.append(targets_rows)
+    n_groups = len(groups)
 
     with ExitStack() as ctx:
+        ctx.enter_context(tc.manual_schedule())
         consts = ctx.enter_context(tc.tile_pool(name="consts", bufs=1))
-        rows = ctx.enter_context(tc.tile_pool(name="rows", bufs=len(groups)))
-        staged = ctx.enter_context(tc.tile_pool(name="staged", bufs=len(groups)))
-        banks = ctx.enter_context(tc.psum_pool(name="banks", bufs=6))
+        rows = ctx.enter_context(tc.tile_pool(name="rows", bufs=n_groups))
+        staged = ctx.enter_context(tc.tile_pool(name="staged", bufs=n_groups))
+        banks = ctx.enter_context(tc.psum_pool(name="banks", bufs=2 * BUNCH))
         sums = ctx.enter_context(tc.psum_pool(name="sums", bufs=1))
 
         w_raw = consts.tile([P, PACK, P], BF16)
-        nc.scalar.dma_start(
-            out=w_raw[:].rearrange("p (u e) l -> p u (e l)", u=HALVES),
-            in_=kernel.rearrange("(u p e) l -> p u (e l)", u=HALVES, e=2),
-        )
         a_sb = consts.tile([P, MEMBERS], BF16)
-        nc.scalar.dma_start(out=a_sb[:], in_=a_rows)
-
         x_tiles = []
-        for group in groups:
-            x = rows.tile([P, group.shape[1]], BF16)
-            nc.sync.dma_start(out=x[:], in_=group)
+        for g in range(n_groups):
+            x = rows.tile([P, groups[g].shape[1]], BF16)
+            nc.sync.dma_start(out=x[:], in_=groups[g])
             x_tiles.append(x)
+            if g == 1:
+                nc.sync.dma_start(
+                    out=w_raw[:].rearrange("p (u e) l -> p u (e l)", u=HALVES),
+                    in_=kernel.rearrange("(u p e) l -> p u (e l)", u=HALVES, e=2),
+                )
+                nc.sync.dma_start(out=a_sb[:], in_=a_rows)
 
         ident = consts.tile([P, P], F32)
         make_identity(nc, ident[:])
+
+        codes_tiles = []
+        scales_tiles = []
+
+        def quantise_group(g):
+            members = x_tiles[g].shape[1] // D
+            x_words = x_tiles[g][:].bitcast(F32)
+
+            xt = banks.tile([P, members, HALVES, P], F32)
+            for m in range(members):
+                for u in range(HALVES):
+                    first_word = (m * HALVES + u) * P
+                    nc.tensor.transpose(
+                        xt[:, m, u, :], x_words[:, first_word : first_word + P], ident[:]
+                    )
+
+            grouped = staged.tile([P, members * P * PACK], BF16, align_bytes=64)
+            nc.scalar.copy(
+                out=grouped[:].bitcast(F32).rearrange("p (m n u) -> p m n u", m=members, u=HALVES),
+                in_=xt[:].rearrange("p m u n -> p m n u"),
+            )
+
+            codes = staged.tile([P, members * P], U32, align_bytes=64)
+            scales = staged.tile([P, members * P], U8, align_bytes=64)
+            nc.vector.quantize_mx(out=codes[:].bitcast(FP8X4), scales=scales[:], in_=grouped[:])
+            codes_tiles.append(codes)
+            scales_tiles.append(scales)
+
+        y = sums.tile([P, P], F32)
+
+        def multiply_group(g):
+            members = x_tiles[g].shape[1] // D
+            for m in range(members):
+                nodes = slice(m * P, (m + 1) * P)
+                nc.tensor.matmul_mx(
+                    out=y[:],
+                    lhsT=codes_tiles[g][:, nodes].bitcast(FP8X4),
+                    lhsT_scale=scales_tiles[g][:, nodes],
+                    rhs=w_codes[:].bitcast(FP8X4),
+                    rhs_scale=w_scales[:],
+                    start=(g == 0 and m == 0),
+                    stop=(g == n_groups - 1 and m == members - 1),
+                )
 
         w_grouped = consts.tile([P, P, PACK], BF16, align_bytes=64)
         nc.vector.tensor_copy(out=w_grouped[:], in_=w_raw[:].rearrange("p t l -> p l t"))
@@ -78,46 +124,11 @@ def tile_singlegcnlayer_s_kernel(tc, targets, neighbors, a, kernel, out):
         inverse = consts.tile([P, 1], F32)
         nc.vector.reciprocal(out=inverse[:], in_=guarded[:])
 
-        y = sums.tile([P, P], F32)
-        passes_done = 0
-        for x in x_tiles:
-            members = x.shape[1] // D
-            x_words = x[:].bitcast(F32)
-
-            xt = banks.tile([P, members, HALVES, P], F32)
-            for m in range(members):
-                for u in range(HALVES):
-                    first_word = (m * HALVES + u) * P
-                    nc.tensor.transpose(
-                        xt[:, m, u, :], x_words[:, first_word : first_word + P], ident[:]
-                    )
-
-            grouped = staged.tile([P, members * P * PACK], BF16, align_bytes=64)
-            grouped_words = grouped[:].bitcast(F32).rearrange(
-                "p (m n u) -> p m n u", m=members, u=HALVES
-            )
-            xt_by_node = xt[:].rearrange("p m u n -> p m n u")
-            if members == BANK_MEMBERS:
-                nc.scalar.copy(out=grouped_words, in_=xt_by_node)
-            else:
-                nc.vector.tensor_copy(out=grouped_words, in_=xt_by_node)
-
-            codes = staged.tile([P, members * P], U32, align_bytes=64)
-            scales = staged.tile([P, members * P], U8, align_bytes=64)
-            nc.vector.quantize_mx(out=codes[:].bitcast(FP8X4), scales=scales[:], in_=grouped[:])
-
-            for m in range(members):
-                nodes = slice(m * P, (m + 1) * P)
-                nc.tensor.matmul_mx(
-                    out=y[:],
-                    lhsT=codes[:, nodes].bitcast(FP8X4),
-                    lhsT_scale=scales[:, nodes],
-                    rhs=w_codes[:].bitcast(FP8X4),
-                    rhs_scale=w_scales[:],
-                    start=(passes_done == 0),
-                    stop=(passes_done == MEMBERS - 1),
-                )
-                passes_done += 1
+        for first in range(0, n_groups + BUNCH, BUNCH):
+            for g in range(first, min(first + BUNCH, n_groups)):
+                quantise_group(g)
+            for g in range(max(first - BUNCH, 0), first):
+                multiply_group(g)
 
         result = consts.tile([P, P], F32)
         nc.vector.tensor_scalar(

@@ -19,6 +19,7 @@ WORDS = D // 2
 HALVES = WORDS // P
 BANK_MEMBERS = 2
 BUNCH = 3
+WARM_UP = 3
 
 FLOPS = 2 * MEMBERS * P * D * P
 
@@ -44,6 +45,7 @@ def tile_singlegcnlayer_s_kernel(tc, targets, neighbors, a, kernel, out):
         staged = ctx.enter_context(tc.tile_pool(name="staged", bufs=n_groups))
         banks = ctx.enter_context(tc.psum_pool(name="banks", bufs=2 * BUNCH))
         sums = ctx.enter_context(tc.psum_pool(name="sums", bufs=1))
+        idle = ctx.enter_context(tc.psum_pool(name="idle", bufs=1))
 
         w_raw = consts.tile([P, PACK, P], BF16)
         a_sb = consts.tile([P, MEMBERS], BF16)
@@ -61,6 +63,14 @@ def tile_singlegcnlayer_s_kernel(tc, targets, neighbors, a, kernel, out):
 
         ident = consts.tile([P, P], F32)
         make_identity(nc, ident[:])
+
+        unread = idle.tile([P, P], F32)
+
+        def keep_busy():
+            nc.tensor.matmul(out=unread[:], lhsT=ident[:], rhs=ident[:], start=True, stop=True)
+
+        for i in range(WARM_UP):
+            keep_busy()
 
         codes_tiles = []
         scales_tiles = []
@@ -127,6 +137,8 @@ def tile_singlegcnlayer_s_kernel(tc, targets, neighbors, a, kernel, out):
         for first in range(0, n_groups + BUNCH, BUNCH):
             for g in range(first, min(first + BUNCH, n_groups)):
                 quantise_group(g)
+                if g < 2 * BUNCH and g % 2 == 1:
+                    keep_busy()
             for g in range(max(first - BUNCH, 0), first):
                 multiply_group(g)
 

@@ -19,7 +19,8 @@ WORDS = D // 2
 HALVES = WORDS // P
 BANK_MEMBERS = 2
 BUNCH = 3
-WARM_UP = 3
+WARM_UP = 4
+IDLE_AFTER = (1, 3)
 
 FLOPS = 2 * MEMBERS * P * D * P
 
@@ -61,13 +62,15 @@ def tile_singlegcnlayer_s_kernel(tc, targets, neighbors, a, kernel, out):
                 )
                 nc.sync.dma_start(out=a_sb[:], in_=a_rows)
 
-        ident = consts.tile([P, P], F32)
-        make_identity(nc, ident[:])
-
+        zeros = consts.tile([P, P], F32)
+        nc.vector.memset(zeros[:], 0.0)
         unread = idle.tile([P, P], F32)
 
         def keep_busy():
-            nc.tensor.matmul(out=unread[:], lhsT=ident[:], rhs=ident[:], start=True, stop=True)
+            nc.tensor.matmul(out=unread[:], lhsT=zeros[:], rhs=zeros[:], start=True, stop=True)
+
+        ident = consts.tile([P, P], F32)
+        make_identity(nc, ident[:])
 
         for i in range(WARM_UP):
             keep_busy()
@@ -137,7 +140,7 @@ def tile_singlegcnlayer_s_kernel(tc, targets, neighbors, a, kernel, out):
         for first in range(0, n_groups + BUNCH, BUNCH):
             for g in range(first, min(first + BUNCH, n_groups)):
                 quantise_group(g)
-                if g < 2 * BUNCH and g % 2 == 1:
+                if g in IDLE_AFTER:
                     keep_busy()
             for g in range(max(first - BUNCH, 0), first):
                 multiply_group(g)

@@ -60,7 +60,7 @@ def tile_singlegcnlayer_s_kernel(tc, targets, neighbors, a, kernel, out):
                     out=w_raw[:].rearrange("p (u e) l -> p u (e l)", u=HALVES),
                     in_=kernel.rearrange("(u p e) l -> p u (e l)", u=HALVES, e=2),
                 )
-                nc.sync.dma_start(out=a_sb[:], in_=a_rows)
+        nc.sync.dma_start(out=a_sb[:], in_=a_rows)
 
         zeros = consts.tile([P, P], F32)
         nc.vector.memset(zeros[:], 0.0)
@@ -128,15 +128,6 @@ def tile_singlegcnlayer_s_kernel(tc, targets, neighbors, a, kernel, out):
             in_=w_grouped[:].rearrange("p l t -> p (l t)"),
         )
 
-        factor = consts.tile([P, 1], F32)
-        nc.vector.tensor_reduce(out=factor[:], in_=a_sb[:], axis=mybir.AxisListType.X, op=ALU.add)
-        small = consts.tile([P, 1], F32)
-        nc.vector.tensor_single_scalar(out=small[:], in_=factor[:], scalar=0.5, op=ALU.is_le)
-        guarded = consts.tile([P, 1], F32)
-        nc.vector.tensor_tensor(out=guarded[:], in0=factor[:], in1=small[:], op=ALU.max)
-        inverse = consts.tile([P, 1], F32)
-        nc.vector.reciprocal(out=inverse[:], in_=guarded[:])
-
         for first in range(0, n_groups + BUNCH, BUNCH):
             for g in range(first, min(first + BUNCH, n_groups)):
                 quantise_group(g)
@@ -144,6 +135,15 @@ def tile_singlegcnlayer_s_kernel(tc, targets, neighbors, a, kernel, out):
                     keep_busy()
             for g in range(max(first - BUNCH, 0), first):
                 multiply_group(g)
+
+        factor = consts.tile([P, 1], F32)
+        nc.vector.tensor_reduce(out=factor[:], in_=a_sb[:], axis=mybir.AxisListType.X, op=ALU.add)
+        guarded = consts.tile([P, 1], F32)
+        nc.vector.scalar_tensor_tensor(
+            out=guarded[:], in0=factor[:], scalar=0.5, in1=factor[:], op0=ALU.is_le, op1=ALU.max
+        )
+        inverse = consts.tile([P, 1], F32)
+        nc.vector.reciprocal(out=inverse[:], in_=guarded[:])
 
         result = consts.tile([P, P], F32)
         nc.vector.tensor_scalar(

@@ -18,9 +18,9 @@ MEMBERS = NEIGHBORS + 1
 WORDS = D // 2
 HALVES = WORDS // P
 BANK_MEMBERS = 2
-BUNCH = 3
+TRANSPOSE_BANKS = 6
 WARM_UP = 4
-IDLE_AFTER = (1, 3)
+IDLE_AFTER = (2, 5)
 
 FLOPS = 2 * MEMBERS * P * D * P
 
@@ -44,7 +44,7 @@ def tile_singlegcnlayer_s_kernel(tc, targets, neighbors, a, kernel, out):
         consts = ctx.enter_context(tc.tile_pool(name="consts", bufs=1))
         rows = ctx.enter_context(tc.tile_pool(name="rows", bufs=n_groups))
         staged = ctx.enter_context(tc.tile_pool(name="staged", bufs=n_groups))
-        banks = ctx.enter_context(tc.psum_pool(name="banks", bufs=2 * BUNCH))
+        banks = ctx.enter_context(tc.psum_pool(name="banks", bufs=TRANSPOSE_BANKS))
         sums = ctx.enter_context(tc.psum_pool(name="sums", bufs=1))
         idle = ctx.enter_context(tc.psum_pool(name="idle", bufs=1))
 
@@ -128,13 +128,12 @@ def tile_singlegcnlayer_s_kernel(tc, targets, neighbors, a, kernel, out):
             in_=w_grouped[:].rearrange("p l t -> p (l t)"),
         )
 
-        for first in range(0, n_groups + BUNCH, BUNCH):
-            for g in range(first, min(first + BUNCH, n_groups)):
-                quantise_group(g)
-                if g in IDLE_AFTER:
-                    keep_busy()
-            for g in range(max(first - BUNCH, 0), first):
-                multiply_group(g)
+        for g in range(n_groups):
+            quantise_group(g)
+            if g in IDLE_AFTER:
+                keep_busy()
+        for g in range(n_groups):
+            multiply_group(g)
 
         factor = consts.tile([P, 1], F32)
         nc.vector.tensor_reduce(out=factor[:], in_=a_sb[:], axis=mybir.AxisListType.X, op=ALU.add)

@@ -19,8 +19,8 @@ WORDS = D // 2
 HALVES = WORDS // P
 BANK_MEMBERS = 2
 TRANSPOSE_BANKS = 6
-WARM_UP = 4
-IDLE_AFTER = (2, 5)
+WARM_UP = 3
+IDLE_AFTER = (1, 3, 5)
 
 FLOPS = 2 * MEMBERS * P * D * P
 

@@ -21,6 +21,7 @@ BANK_MEMBERS = 2
 TRANSPOSE_BANKS = 6
 WARM_UP = 3
 IDLE_AFTER = (1, 3, 5)
+SINGLES = 3
 
 FLOPS = 2 * MEMBERS * P * D * P
 
@@ -32,12 +33,15 @@ def tile_singlegcnlayer_s_kernel(tc, targets, neighbors, a, kernel, out):
     a_rows = a.rearrange("b n k -> (b n) k")
     out_rows = out.rearrange("b n l -> (b n) l")
 
+    paired = NEIGHBORS - (SINGLES - 1)
     groups = [
         neighbor_rows[:, first * D : (first + BANK_MEMBERS) * D]
-        for first in range(0, NEIGHBORS, BANK_MEMBERS)
+        for first in range(0, paired, BANK_MEMBERS)
     ]
+    groups.extend([neighbor_rows[:, k * D : (k + 1) * D] for k in range(paired, NEIGHBORS)])
     groups.append(targets_rows)
     n_groups = len(groups)
+    vector_copies = n_groups - SINGLES
 
     with ExitStack() as ctx:
         ctx.enter_context(tc.manual_schedule())
@@ -78,7 +82,9 @@ def tile_singlegcnlayer_s_kernel(tc, targets, neighbors, a, kernel, out):
         codes_tiles = []
         scales_tiles = []
 
-        def quantise_group(g):
+        grouped_tiles = []
+
+        def transpose_group(g):
             members = x_tiles[g].shape[1] // D
             x_words = x_tiles[g][:].bitcast(F32)
 
@@ -91,14 +97,20 @@ def tile_singlegcnlayer_s_kernel(tc, targets, neighbors, a, kernel, out):
                     )
 
             grouped = staged.tile([P, members * P * PACK], BF16, align_bytes=64)
-            nc.scalar.copy(
+            copy_out = nc.vector.tensor_copy if g == vector_copies else nc.scalar.copy
+            copy_out(
                 out=grouped[:].bitcast(F32).rearrange("p (m n u) -> p m n u", m=members, u=HALVES),
                 in_=xt[:].rearrange("p m u n -> p m n u"),
             )
+            grouped_tiles.append(grouped)
 
+        def quantise_group(g):
+            members = x_tiles[g].shape[1] // D
             codes = staged.tile([P, members * P], U32, align_bytes=64)
             scales = staged.tile([P, members * P], U8, align_bytes=64)
-            nc.vector.quantize_mx(out=codes[:].bitcast(FP8X4), scales=scales[:], in_=grouped[:])
+            nc.vector.quantize_mx(
+                out=codes[:].bitcast(FP8X4), scales=scales[:], in_=grouped_tiles[g][:]
+            )
             codes_tiles.append(codes)
             scales_tiles.append(scales)
 
@@ -129,9 +141,12 @@ def tile_singlegcnlayer_s_kernel(tc, targets, neighbors, a, kernel, out):
         )
 
         for g in range(n_groups):
-            quantise_group(g)
+            transpose_group(g)
             if g in IDLE_AFTER:
                 keep_busy()
+            if g > 0:
+                quantise_group(g - 1)
+        quantise_group(n_groups - 1)
         for g in range(n_groups):
             multiply_group(g)
 

@@ -53,17 +53,16 @@ def tile_singlegcnlayer_s_kernel(tc, targets, neighbors, a, kernel, out):
         idle = ctx.enter_context(tc.psum_pool(name="idle", bufs=1))
 
         w_raw = consts.tile([P, PACK, P], BF16)
+        nc.scalar.dma_start(
+            out=w_raw[:].rearrange("p (u e) l -> p u (e l)", u=HALVES),
+            in_=kernel.rearrange("(u p e) l -> p u (e l)", u=HALVES, e=2),
+        )
         a_sb = consts.tile([P, MEMBERS], BF16)
         x_tiles = []
         for g in range(n_groups):
             x = rows.tile([P, groups[g].shape[1]], BF16)
             nc.sync.dma_start(out=x[:], in_=groups[g])
             x_tiles.append(x)
-            if g == 1:
-                nc.sync.dma_start(
-                    out=w_raw[:].rearrange("p (u e) l -> p u (e l)", u=HALVES),
-                    in_=kernel.rearrange("(u p e) l -> p u (e l)", u=HALVES, e=2),
-                )
         nc.sync.dma_start(out=a_sb[:], in_=a_rows)
 
         zeros = consts.tile([P, P], F32)

@@ -20,7 +20,7 @@ HALVES = WORDS // P
 BANK_MEMBERS = 2
 TRANSPOSE_BANKS = 6
 WARM_UP = 3
-IDLE_AFTER = (1, 3, 5)
+IDLE_AFTER = (2, 4, 6)
 SINGLES = 3
 
 FLOPS = 2 * MEMBERS * P * D * P

@@ -22,6 +22,7 @@ TRANSPOSE_BANKS = 6
 WARM_UP = 3
 IDLE_AFTER = (2, 4, 6)
 SINGLES = 3
+EARLY_VECTOR_COPY = 3
 
 FLOPS = 2 * MEMBERS * P * D * P
 
@@ -41,7 +42,7 @@ def tile_singlegcnlayer_s_kernel(tc, targets, neighbors, a, kernel, out):
     groups.extend([neighbor_rows[:, k * D : (k + 1) * D] for k in range(paired, NEIGHBORS)])
     groups.append(targets_rows)
     n_groups = len(groups)
-    vector_copies = n_groups - SINGLES
+    vector_copies = (EARLY_VECTOR_COPY, n_groups - SINGLES)
 
     with ExitStack() as ctx:
         ctx.enter_context(tc.manual_schedule())
@@ -96,7 +97,7 @@ def tile_singlegcnlayer_s_kernel(tc, targets, neighbors, a, kernel, out):
                     )
 
             grouped = staged.tile([P, members * P * PACK], BF16, align_bytes=64)
-            copy_out = nc.vector.tensor_copy if g == vector_copies else nc.scalar.copy
+            copy_out = nc.vector.tensor_copy if g in vector_copies else nc.scalar.copy
             copy_out(
                 out=grouped[:].bitcast(F32).rearrange("p (m n u) -> p m n u", m=members, u=HALVES),
                 in_=xt[:].rearrange("p m u n -> p m n u"),

from contextlib import ExitStack

import concourse.mybir as mybir
from concourse.masks import make_identity

F32 = mybir.dt.float32
BF16 = mybir.dt.bfloat16
U32 = mybir.dt.uint32
U8 = mybir.dt.uint8
FP8X4 = mybir.dt.float8_e4m3fn_x4
ALU = mybir.AluOpType

P = 128
D = 512
PACK = 4
NEIGHBORS = 16
MEMBERS = NEIGHBORS + 1
WORDS = D // 2
HALVES = WORDS // P
BANK_MEMBERS = 2
TRANSPOSE_BANKS = 6
WARM_UP = 3
IDLE_AFTER = (2, 4, 6)
SINGLES = 3
EARLY_VECTOR_COPY = 3

FLOPS = 2 * MEMBERS * P * D * P


def tile_singlegcnlayer_s_kernel(tc, targets, neighbors, a, kernel, out):
    nc = tc.nc
    targets_rows = targets.rearrange("b n d -> (b n) d")
    neighbor_rows = neighbors.rearrange("b n k d -> (b n) (k d)")
    a_rows = a.rearrange("b n k -> (b n) k")
    out_rows = out.rearrange("b n l -> (b n) l")

    paired = NEIGHBORS - (SINGLES - 1)
    groups = [
        neighbor_rows[:, first * D : (first + BANK_MEMBERS) * D]
        for first in range(0, paired, BANK_MEMBERS)
    ]
    groups.extend([neighbor_rows[:, k * D : (k + 1) * D] for k in range(paired, NEIGHBORS)])
    groups.append(targets_rows)
    n_groups = len(groups)
    vector_copies = (EARLY_VECTOR_COPY, n_groups - SINGLES)

    with ExitStack() as ctx:
        ctx.enter_context(tc.manual_schedule())
        consts = ctx.enter_context(tc.tile_pool(name="consts", bufs=1))
        rows = ctx.enter_context(tc.tile_pool(name="rows", bufs=n_groups))
        staged = ctx.enter_context(tc.tile_pool(name="staged", bufs=n_groups))
        banks = ctx.enter_context(tc.psum_pool(name="banks", bufs=TRANSPOSE_BANKS))
        sums = ctx.enter_context(tc.psum_pool(name="sums", bufs=1))
        idle = ctx.enter_context(tc.psum_pool(name="idle", bufs=1))

        w_raw = consts.tile([P, PACK, P], BF16)
        nc.scalar.dma_start(
            out=w_raw[:].rearrange("p (u e) l -> p u (e l)", u=HALVES),
            in_=kernel.rearrange("(u p e) l -> p u (e l)", u=HALVES, e=2),
        )
        a_sb = consts.tile([P, MEMBERS], BF16)
        x_tiles = []
        for g in range(n_groups):
            x = rows.tile([P, groups[g].shape[1]], BF16)
            nc.sync.dma_start(out=x[:], in_=groups[g])
            x_tiles.append(x)
        nc.sync.dma_start(out=a_sb[:], in_=a_rows)

        zeros = consts.tile([P, P], F32)
        nc.vector.memset(zeros[:], 0.0)
        unread = idle.tile([P, P], F32)

        def keep_busy():
            nc.tensor.matmul(out=unread[:], lhsT=zeros[:], rhs=zeros[:], start=True, stop=True)

        ident = consts.tile([P, P], F32)
        make_identity(nc, ident[:])

        for i in range(WARM_UP):
            keep_busy()

        codes_tiles = []
        scales_tiles = []

        grouped_tiles = []

        def transpose_group(g):
            members = x_tiles[g].shape[1] // D
            x_words = x_tiles[g][:].bitcast(F32)

            xt = banks.tile([P, members, HALVES, P], F32)
            for m in range(members):
                for u in range(HALVES):
                    first_word = (m * HALVES + u) * P
                    nc.tensor.transpose(
                        xt[:, m, u, :], x_words[:, first_word : first_word + P], ident[:]
                    )

            grouped = staged.tile([P, members * P * PACK], BF16, align_bytes=64)
            copy_out = nc.vector.tensor_copy if g in vector_copies else nc.scalar.copy
            copy_out(
                out=grouped[:].bitcast(F32).rearrange("p (m n u) -> p m n u", m=members, u=HALVES),
                in_=xt[:].rearrange("p m u n -> p m n u"),
            )
            grouped_tiles.append(grouped)

        def quantise_group(g):
            members = x_tiles[g].shape[1] // D
            codes = staged.tile([P, members * P], U32, align_bytes=64)
            scales = staged.tile([P, members * P], U8, align_bytes=64)
            nc.vector.quantize_mx(
                out=codes[:].bitcast(FP8X4), scales=scales[:], in_=grouped_tiles[g][:]
            )
            codes_tiles.append(codes)
            scales_tiles.append(scales)

        y = sums.tile([P, P], F32)

        def multiply_group(g):
            members = x_tiles[g].shape[1] // D
            for m in range(members):
                nodes = slice(m * P, (m + 1) * P)
                nc.tensor.matmul_mx(
                    out=y[:],
                    lhsT=codes_tiles[g][:, nodes].bitcast(FP8X4),
                    lhsT_scale=scales_tiles[g][:, nodes],
                    rhs=w_codes[:].bitcast(FP8X4),
                    rhs_scale=w_scales[:],
                    start=(g == 0 and m == 0),
                    stop=(g == n_groups - 1 and m == members - 1),
                )

        w_grouped = consts.tile([P, P, PACK], BF16, align_bytes=64)
        nc.vector.tensor_copy(out=w_grouped[:], in_=w_raw[:].rearrange("p t l -> p l t"))
        w_codes = consts.tile([P, P], U32, align_bytes=64)
        w_scales = consts.tile([P, P], U8, align_bytes=64)
        nc.vector.quantize_mx(
            out=w_codes[:].bitcast(FP8X4),
            scales=w_scales[:],
            in_=w_grouped[:].rearrange("p l t -> p (l t)"),
        )

        for g in range(n_groups):
            transpose_group(g)
            if g in IDLE_AFTER:
                keep_busy()
            if g > 0:
                quantise_group(g - 1)
        quantise_group(n_groups - 1)
        for g in range(n_groups):
            multiply_group(g)

        factor = consts.tile([P, 1], F32)
        nc.vector.tensor_reduce(out=factor[:], in_=a_sb[:], axis=mybir.AxisListType.X, op=ALU.add)
        guarded = consts.tile([P, 1], F32)
        nc.vector.scalar_tensor_tensor(
            out=guarded[:], in0=factor[:], scalar=0.5, in1=factor[:], op0=ALU.is_le, op1=ALU.max
        )
        inverse = consts.tile([P, 1], F32)
        nc.vector.reciprocal(out=inverse[:], in_=guarded[:])

        result = consts.tile([P, P], F32)
        nc.vector.tensor_scalar(
            out=result[:], in0=y[:], scalar1=inverse[:, 0:1], scalar2=0.0, op0=ALU.mult, op1=ALU.max
        )
        nc.sync.dma_start(out=out_rows, in_=result[:])
